import numpy as np
import ml_dtypes


def mxq(x, axis, fmt="e4m3"):
    dtype, down = {"e4m3": (ml_dtypes.float8_e4m3fn, 7), "e5m2": (ml_dtypes.float8_e5m2, 14)}[fmt]
    v = np.moveaxis(np.asarray(x, np.float32).astype(ml_dtypes.bfloat16).astype(np.float64), axis, -1)
    blocks = v.reshape(v.shape[:-1] + (-1, 32))
    amax = np.abs(blocks).max(-1, keepdims=True)
    byte = np.maximum(np.where(amax > 0, np.frexp(amax)[1] - 1 + 127, 0) - down, 1)
    scale = np.exp2(byte - 127.0)
    codes = (blocks / scale).astype(np.float32).astype(dtype).astype(np.float64)
    return np.moveaxis((codes * scale).reshape(v.shape), -1, axis)


WIDE = False


def mx_kscale(k):
    if not WIDE:
        return np.ones(k)
    levels = np.array([10, -10, 5, -5, 0])
    a = np.random.permutation(np.resize(levels, k // 512 * 4)).reshape(k // 512, 4)
    idx = np.arange(k)
    return np.exp2(a[idx // 512, idx % 128 // 32])


BF16 = ml_dtypes.bfloat16


def bf(x):
    return np.asarray(x, np.float32).astype(BF16)


def f64(x):
    return np.asarray(x).astype(np.float64)


E2M1 = np.array([0.0, 0.5, 1.0, 1.5, 2.0, 3.0, 4.0, 6.0, -0.0, -0.5, -1.0, -1.5, -2.0, -3.0, -4.0, -6.0])


def pack_weight(w, fmt):
    k, n = w.shape
    w = f64(bf(w)).reshape(k // 32, 32, n)
    amax = np.abs(w).max(1)
    if fmt == "e4m3":
        byte = np.frexp(amax)[1] - 1 + 127 - 7
    else:
        mant, ex = np.frexp(amax / 6.0)
        byte = np.where(mant > 0.5, ex, ex - 1) + 127
    byte = np.clip(np.where(amax > 0, byte, 1), 1, 254)
    scaled = (w * np.exp2(127.0 - byte)[:, None, :]).reshape(k, n).astype(np.float32)
    by_word = np.ascontiguousarray(scaled.reshape(k // 512, 128, 4, n).transpose(0, 1, 3, 2))
    if fmt == "e4m3":
        words = by_word.astype(ml_dtypes.float8_e4m3fn).view(np.uint8)
    else:
        c = by_word.astype(ml_dtypes.float4_e2m1fn).view(np.uint8) & 0xF
        words = c[..., 0::2] | (c[..., 1::2] << 4)
    return np.ascontiguousarray(words), np.ascontiguousarray(byte.astype(np.uint8).reshape(k // 512, 16, n))


def unpack_weight(words, scales, fmt):
    g, p, n, _ = words.shape
    if fmt == "e4m3":
        vals = np.ascontiguousarray(words).view(ml_dtypes.float8_e4m3fn).astype(np.float64)
    else:
        nib = np.empty((g, p, n, 4), np.uint8)
        nib[..., 0::2] = words & 0xF
        nib[..., 1::2] = words >> 4
        vals = E2M1[nib]
    vals = vals * np.repeat(np.exp2(scales.astype(np.float64) - 127.0), 8, axis=1)[..., None]
    return vals.transpose(0, 1, 3, 2).reshape(g * 512, n)


B, S, D, H, KV, HD = 2, 2048, 1024, 4, 2, 128
HALF = HD // 2
ROPE_BASE = 1.0e4
FMT = "e4m3"


def rotate_half(t):
    return np.concatenate((-t[..., HALF:], t[..., :HALF]), axis=-1)


def setup_inputs():
    s = mx_kscale(D)
    inv_freq = 1.0 / ROPE_BASE ** (np.arange(HALF) / HALF)
    freqs = np.outer(np.arange(S), inv_freq)
    emb = np.concatenate((freqs, freqs), axis=-1)
    w = 1.0 / np.sqrt(D)
    x = bf(np.random.standard_normal((B, S, D)) * s)
    Wq_words, Wq_scales = pack_weight(np.random.standard_normal((D, H * HD)) * w / s[:, None], FMT)
    Wk_words, Wk_scales = pack_weight(np.random.standard_normal((D, KV * HD)) * w / s[:, None], FMT)
    Wv_words, Wv_scales = pack_weight(np.random.standard_normal((D, KV * HD)) * w / s[:, None], FMT)
    return {"x": x,
            "cos": bf(np.cos(emb)),
            "sin": bf(np.sin(emb)),
            "Wq_words": Wq_words,
            "Wq_scales": Wq_scales,
            "Wk_words": Wk_words,
            "Wk_scales": Wk_scales,
            "Wv_words": Wv_words,
            "Wv_scales": Wv_scales}


def reference(x, cos, sin, Wq_words, Wq_scales, Wk_words, Wk_scales, Wv_words, Wv_scales):
    xq = mxq(f64(x), 2, "e4m3")
    q = (xq @ unpack_weight(Wq_words, Wq_scales, FMT)).reshape(B, S, H, HD)
    k = (xq @ unpack_weight(Wk_words, Wk_scales, FMT)).reshape(B, S, KV, HD)
    v = (xq @ unpack_weight(Wv_words, Wv_scales, FMT)).reshape(B, S, KV, HD)
    c = f64(cos)[None, :, None, :]
    sn = f64(sin)[None, :, None, :]
    q_rot = q * c + rotate_half(q) * sn
    k_rot = k * c + rotate_half(k) * sn
    return q_rot, k_rot, v

@@ -1,0 +1,192 @@
+import concourse.mybir as mybir
+from concourse.masks import make_identity
+
+F32 = mybir.dt.float32
+BF16 = mybir.dt.bfloat16
+I32 = mybir.dt.int32
+U32 = mybir.dt.uint32
+U8 = mybir.dt.uint8
+FP8X4 = mybir.dt.float8_e4m3fn_x4
+MULT = mybir.AluOpType.mult
+ADD = mybir.AluOpType.add
+
+P = 128
+BATCH, SEQ, D = 2, 2048, 1024
+HEAD = 128
+HALF = HEAD // 2
+Q_HEADS, KV_HEADS = 4, 2
+Q_COLS = Q_HEADS * HEAD
+KV_COLS = KV_HEADS * HEAD
+W_COLS = Q_COLS + 2 * KV_COLS
+BANK = 512
+K_PASS = 4 * P
+PASSES = D // K_PASS
+WORDS = K_PASS // 2
+
+CHUNK_TILES = 4
+CHUNKS = BATCH * SEQ // (P * CHUNK_TILES)
+SEQ_CHUNKS = SEQ // (P * CHUNK_TILES)
+PAIR = 2
+PAIRS = CHUNKS * CHUNK_TILES // PAIR
+
+FLOPS = 2 * BATCH * SEQ * D * W_COLS
+
+
+def tile_attention_pa_t_kernel(
+    tc, x, cos, sin, Wq_words, Wq_scales, Wk_words, Wk_scales, Wv_words, Wv_scales, out_0, out_1, out_2
+):
+    nc = tc.nc
+
+    x_chunks = x.rearrange("b (c p j) d -> (b c) p j d", p=P, j=CHUNK_TILES)
+    q_chunks = out_0.rearrange("b (c p j) h d -> (b c) p j (h d)", p=P, j=CHUNK_TILES)
+    k_chunks = out_1.rearrange("b (c p j) h d -> (b c) p j (h d)", p=P, j=CHUNK_TILES)
+    v_chunks = out_2.rearrange("b (c p j) h d -> (b c) p j (h d)", p=P, j=CHUNK_TILES)
+
+    with tc.tile_pool(name="fixed", bufs=1) as fixed, tc.tile_pool(name="xin", bufs=PAIRS) as xin, tc.tile_pool(
+        name="quant", bufs=2
+    ) as quant, tc.tile_pool(name="work", bufs=3) as work, tc.tile_pool(name="result", bufs=3) as result, tc.psum_pool(
+        name="flip", bufs=2
+    ) as flip, tc.psum_pool(name="sums", bufs=3) as sums, tc.manual_schedule():
+        w_codes = fixed.tile([P, PASSES, W_COLS], U32, align_bytes=64)
+        w_planes = fixed.tile([P, PASSES, W_COLS], U8, align_bytes=64)
+        nc.vector.memset(w_planes[:].rearrange("p g n -> p (g n)").bitcast(I32), 0)
+
+        identity = fixed.tile([P, P], F32)
+        make_identity(nc, identity[:])
+        weights = (
+            (Wq_words, Wq_scales, 0, Q_COLS),
+            (Wk_words, Wk_scales, Q_COLS, KV_COLS),
+            (Wv_words, Wv_scales, Q_COLS + KV_COLS, KV_COLS),
+        )
+        for w_words, w_scales, start, width in weights:
+            nc.gpsimd.dma_start(
+                out=w_codes[:, :, start : start + width].bitcast(F32),
+                in_=w_words.rearrange("g p n t -> p g (n t)").bitcast(F32),
+            )
+
+        x_tiles = []
+        for n in range(PAIRS):
+            x_tile = xin.tile([P, PAIR, D], BF16)
+            x_tiles.append(x_tile)
+
+        def load_x(n):
+            first = PAIR * (n % 2)
+            nc.sync.dma_start(out=x_tiles[n][:], in_=x_chunks[n // 2][:, first : first + PAIR, :])
+
+        load_x(0)
+        load_x(1)
+        loaded = 2
+        for w_words, w_scales, start, width in weights:
+            rows = w_scales.rearrange("g (q r) n -> r q g n", r=4)
+            for r in range(4):
+                nc.sync.dma_start(
+                    out=w_planes[r:P:32, :, start : start + width].bitcast(I32), in_=rows[r].bitcast(I32)
+                )
+            load_x(loaded)
+            loaded += 1
+        cos_sb = fixed.tile([P, SEQ_CHUNKS, CHUNK_TILES, HEAD], BF16)
+        sin_sb = fixed.tile([P, SEQ_CHUNKS, CHUNK_TILES, HEAD], BF16)
+        nc.sync.dma_start(out=cos_sb[:], in_=cos.rearrange("(c p j) d -> p c j d", p=P, j=CHUNK_TILES))
+        nc.sync.dma_start(out=sin_sb[:], in_=sin.rearrange("(c p j) d -> p c j d", p=P, j=CHUNK_TILES))
+        for n in range(loaded, PAIRS):
+            load_x(n)
+
+        operand_of = {}
+        result_of = {}
+
+        def quantise_pair(n):
+            grouped = quant.tile([P, PAIR, PASSES, P, 4], BF16, align_bytes=64)
+            flipped = []
+            for i in range(PAIR):
+                words = x_tiles[n][:, i, :].bitcast(F32)
+                xt = flip.tile([P, PASSES, 2, P], F32)
+                flipped.append(xt)
+                for g in range(PASSES):
+                    for u in range(2):
+                        nc.tensor.transpose(xt[:, g, u, :], words[:, WORDS * g + u : WORDS * (g + 1) : 2], identity[:])
+            for i in range(PAIR):
+                nc.scalar.copy(out=grouped[:, i].bitcast(F32), in_=flipped[i][:].rearrange("p g u r -> p g r u"))
+            codes = quant.tile([P, PAIR, PASSES, P], U32, align_bytes=64)
+            planes = quant.tile([P, PAIR, PASSES, P], U8, align_bytes=64)
+            operand_of[n] = (codes, planes)
+            nc.vector.quantize_mx(
+                out=codes[:].rearrange("p i g r -> p (i g r)").bitcast(FP8X4),
+                scales=planes[:].rearrange("p i g r -> p (i g r)"),
+                in_=grouped[:].rearrange("p i g r t -> p (i g r t)"),
+            )
+
+        def times_cos(sums_cols, heads, cos_row, straight):
+            nc.vector.tensor_tensor(
+                out=straight.rearrange("p (h d) -> p h d", h=heads),
+                in0=sums_cols.rearrange("p (h d) -> p h d", h=heads),
+                in1=cos_row.unsqueeze(1).to_broadcast([P, heads, HEAD]),
+                op=MULT,
+            )
+
+        def times_sin(sums_cols, heads, sin_row, cross, s):
+            u = sums_cols.rearrange("p (h s d) -> p h s d", h=heads, s=2)
+            nc.vector.scalar_tensor_tensor(
+                out=cross.rearrange("p (h s d) -> p h s d", h=heads, s=2)[:, :, s, :],
+                in0=u[:, :, 1 - s, :],
+                scalar=(-1.0 if s == 0 else 1.0),
+                in1=sin_row[:, HALF * s : HALF * (s + 1)].unsqueeze(1).to_broadcast([P, heads, HALF]),
+                op0=MULT,
+                op1=MULT,
+            )
+
+        def store_rows(c, first, count):
+            q_out, k_out, v_out = result_of[c]
+            nc.sync.dma_start(out=q_chunks[c][:, first : first + count, :], in_=q_out[:, first : first + count, :])
+            nc.sync.dma_start(out=k_chunks[c][:, first : first + count, :], in_=k_out[:, first : first + count, :])
+            nc.sync.dma_start(out=v_chunks[c][:, first : first + count, :], in_=v_out[:, first : first + count, :])
+
+        def project_pair(n):
+            codes, planes = operand_of[n]
+            c = n // 2
+            first = PAIR * (n % 2)
+            if first == 0:
+                q_new = result.tile([P, CHUNK_TILES, Q_COLS], F32)
+                k_new = result.tile([P, CHUNK_TILES, KV_COLS], F32)
+                v_new = result.tile([P, CHUNK_TILES, KV_COLS], F32)
+                result_of[c] = (q_new, k_new, v_new)
+            q_out, k_out, v_out = result_of[c]
+            for i in range(PAIR):
+                j = first + i
+                sums_q = sums.tile([P, BANK], F32)
+                sums_kv = sums.tile([P, BANK], F32)
+                for acc, start in ((sums_kv, Q_COLS), (sums_q, 0)):
+                    for g in range(PASSES):
+                        nc.tensor.matmul_mx(
+                            out=acc[:],
+                            lhsT=codes[:, i, g, :].bitcast(FP8X4),
+                            lhsT_scale=planes[:, i, g, :],
+                            rhs=w_codes[:, g, start : start + BANK].bitcast(FP8X4),
+                            rhs_scale=w_planes[:, g, start : start + BANK],
+                            start=(g == 0),
+                            stop=(g == PASSES - 1),
+                        )
+                nc.scalar.copy(out=v_out[:, j, :], in_=sums_kv[:, KV_COLS:BANK])
+                cos_row = cos_sb[:, c % SEQ_CHUNKS, j, :]
+                sin_row = sin_sb[:, c % SEQ_CHUNKS, j, :]
+                cross_q = work.tile([P, Q_COLS], F32)
+                cross_k = work.tile([P, KV_COLS], F32)
+                keys = sums_kv[:, 0:KV_COLS]
+                times_cos(keys, KV_HEADS, cos_row, k_out[:, j, :])
+                times_sin(keys, KV_HEADS, sin_row, cross_k[:], 0)
+                times_sin(keys, KV_HEADS, sin_row, cross_k[:], 1)
+                times_cos(sums_q[:], Q_HEADS, cos_row, q_out[:, j, :])
+                times_sin(sums_q[:], Q_HEADS, sin_row, cross_q[:], 0)
+                nc.vector.tensor_tensor(out=k_out[:, j, :], in0=k_out[:, j, :], in1=cross_k[:], op=ADD)
+                times_sin(sums_q[:], Q_HEADS, sin_row, cross_q[:], 1)
+                nc.gpsimd.tensor_tensor(out=q_out[:, j, :], in0=q_out[:, j, :], in1=cross_q[:], op=ADD)
+            if c == CHUNKS - 1:
+                store_rows(c, first, PAIR)
+            elif first + PAIR == CHUNK_TILES:
+                store_rows(c, 0, CHUNK_TILES)
+
+        quantise_pair(0)
+        quantise_pair(1)
+        for n in range(PAIRS):
+            project_pair(n)
+            if n + 2 < PAIRS:
+                quantise_pair(n + 2)

@@ -46,7 +46,9 @@ def tile_attention_pa_t_kernel(
         name="quant", bufs=2
     ) as quant, tc.tile_pool(name="work", bufs=3) as work, tc.tile_pool(name="result", bufs=3) as result, tc.psum_pool(
         name="flip", bufs=2
-    ) as flip, tc.psum_pool(name="sums", bufs=3) as sums, tc.manual_schedule():
+    ) as flip, tc.psum_pool(name="qsum", bufs=3) as qsum, tc.psum_pool(name="ksum", bufs=2) as ksum, tc.psum_pool(
+        name="vsum", bufs=1
+    ) as vsum, tc.manual_schedule():
         w_codes = fixed.tile([P, PASSES, W_COLS], U32, align_bytes=64)
         w_planes = fixed.tile([P, PASSES, W_COLS], U8, align_bytes=64)
         nc.vector.memset(w_planes[:].rearrange("p g n -> p (g n)").bitcast(I32), 0)
@@ -90,12 +92,17 @@ def tile_attention_pa_t_kernel(
         nc.sync.dma_start(out=sin_sb[:], in_=sin.rearrange("(c p j) d -> p c j d", p=P, j=CHUNK_TILES))
         for n in range(loaded, PAIRS):
             load_x(n)
+        nc.gpsimd.tensor_scalar(
+            out=sin_sb[:, :, :, 0:HALF], in0=sin_sb[:, :, :, 0:HALF], scalar1=-1.0, scalar2=0.0, op0=MULT, op1=ADD
+        )
 
+        grouped_of = {}
         operand_of = {}
         result_of = {}
 
-        def quantise_pair(n):
+        def flip_pair(n):
             grouped = quant.tile([P, PAIR, PASSES, P, 4], BF16, align_bytes=64)
+            grouped_of[n] = grouped
             flipped = []
             for i in range(PAIR):
                 words = x_tiles[n][:, i, :].bitcast(F32)
@@ -106,39 +113,22 @@ def tile_attention_pa_t_kernel(
                         nc.tensor.transpose(xt[:, g, u, :], words[:, WORDS * g + u : WORDS * (g + 1) : 2], identity[:])
             for i in range(PAIR):
                 nc.scalar.copy(out=grouped[:, i].bitcast(F32), in_=flipped[i][:].rearrange("p g u r -> p g r u"))
+
+        def quantise_pair(n):
             codes = quant.tile([P, PAIR, PASSES, P], U32, align_bytes=64)
             planes = quant.tile([P, PAIR, PASSES, P], U8, align_bytes=64)
             operand_of[n] = (codes, planes)
             nc.vector.quantize_mx(
                 out=codes[:].rearrange("p i g r -> p (i g r)").bitcast(FP8X4),
                 scales=planes[:].rearrange("p i g r -> p (i g r)"),
-                in_=grouped[:].rearrange("p i g r t -> p (i g r t)"),
-            )
-
-        def times_cos(sums_cols, heads, cos_row, straight):
-            nc.vector.tensor_tensor(
-                out=straight.rearrange("p (h d) -> p h d", h=heads),
-                in0=sums_cols.rearrange("p (h d) -> p h d", h=heads),
-                in1=cos_row.unsqueeze(1).to_broadcast([P, heads, HEAD]),
-                op=MULT,
-            )
-
-        def times_sin(sums_cols, heads, sin_row, cross, s):
-            u = sums_cols.rearrange("p (h s d) -> p h s d", h=heads, s=2)
-            nc.vector.scalar_tensor_tensor(
-                out=cross.rearrange("p (h s d) -> p h s d", h=heads, s=2)[:, :, s, :],
-                in0=u[:, :, 1 - s, :],
-                scalar=(-1.0 if s == 0 else 1.0),
-                in1=sin_row[:, HALF * s : HALF * (s + 1)].unsqueeze(1).to_broadcast([P, heads, HALF]),
-                op0=MULT,
-                op1=MULT,
+                in_=grouped_of[n][:].rearrange("p i g r t -> p (i g r t)"),
             )
 
         def store_rows(c, first, count):
             q_out, k_out, v_out = result_of[c]
-            nc.sync.dma_start(out=q_chunks[c][:, first : first + count, :], in_=q_out[:, first : first + count, :])
-            nc.sync.dma_start(out=k_chunks[c][:, first : first + count, :], in_=k_out[:, first : first + count, :])
             nc.sync.dma_start(out=v_chunks[c][:, first : first + count, :], in_=v_out[:, first : first + count, :])
+            nc.sync.dma_start(out=k_chunks[c][:, first : first + count, :], in_=k_out[:, first : first + count, :])
+            nc.sync.dma_start(out=q_chunks[c][:, first : first + count, :], in_=q_out[:, first : first + count, :])
 
         def project_pair(n):
             codes, planes = operand_of[n]
@@ -150,43 +140,85 @@ def tile_attention_pa_t_kernel(
                 v_new = result.tile([P, CHUNK_TILES, KV_COLS], F32)
                 result_of[c] = (q_new, k_new, v_new)
             q_out, k_out, v_out = result_of[c]
+
+            def passes(acc, i, start, width):
+                for g in range(PASSES):
+                    nc.tensor.matmul_mx(
+                        out=acc,
+                        lhsT=codes[:, i, g, :].bitcast(FP8X4),
+                        lhsT_scale=planes[:, i, g, :],
+                        rhs=w_codes[:, g, start : start + width].bitcast(FP8X4),
+                        rhs_scale=w_planes[:, g, start : start + width],
+                        start=(g == 0),
+                        stop=(g == PASSES - 1),
+                    )
+
+            sums_k = ksum.tile([P, PAIR, KV_COLS], F32)
+            sums_v = vsum.tile([P, PAIR, KV_COLS], F32)
+            sums_q = []
             for i in range(PAIR):
-                j = first + i
-                sums_q = sums.tile([P, BANK], F32)
-                sums_kv = sums.tile([P, BANK], F32)
-                for acc, start in ((sums_kv, Q_COLS), (sums_q, 0)):
-                    for g in range(PASSES):
-                        nc.tensor.matmul_mx(
-                            out=acc[:],
-                            lhsT=codes[:, i, g, :].bitcast(FP8X4),
-                            lhsT_scale=planes[:, i, g, :],
-                            rhs=w_codes[:, g, start : start + BANK].bitcast(FP8X4),
-                            rhs_scale=w_planes[:, g, start : start + BANK],
-                            start=(g == 0),
-                            stop=(g == PASSES - 1),
-                        )
-                nc.scalar.copy(out=v_out[:, j, :], in_=sums_kv[:, KV_COLS:BANK])
-                cos_row = cos_sb[:, c % SEQ_CHUNKS, j, :]
-                sin_row = sin_sb[:, c % SEQ_CHUNKS, j, :]
-                cross_q = work.tile([P, Q_COLS], F32)
-                cross_k = work.tile([P, KV_COLS], F32)
-                keys = sums_kv[:, 0:KV_COLS]
-                times_cos(keys, KV_HEADS, cos_row, k_out[:, j, :])
-                times_sin(keys, KV_HEADS, sin_row, cross_k[:], 0)
-                times_sin(keys, KV_HEADS, sin_row, cross_k[:], 1)
-                times_cos(sums_q[:], Q_HEADS, cos_row, q_out[:, j, :])
-                times_sin(sums_q[:], Q_HEADS, sin_row, cross_q[:], 0)
-                nc.vector.tensor_tensor(out=k_out[:, j, :], in0=k_out[:, j, :], in1=cross_k[:], op=ADD)
-                times_sin(sums_q[:], Q_HEADS, sin_row, cross_q[:], 1)
-                nc.gpsimd.tensor_tensor(out=q_out[:, j, :], in0=q_out[:, j, :], in1=cross_q[:], op=ADD)
+                passes(sums_k[:, i, :], i, Q_COLS, KV_COLS)
+            for i in range(PAIR):
+                sums_qi = qsum.tile([P, Q_COLS], F32)
+                sums_q.append(sums_qi)
+                passes(sums_qi[:], i, 0, Q_COLS)
+            for i in range(PAIR):
+                passes(sums_v[:, i, :], i, Q_COLS + KV_COLS, KV_COLS)
+            nc.scalar.copy(out=v_out[:, first : first + PAIR, :], in_=sums_v[:])
+            if n + 2 < PAIRS:
+                flip_pair(n + 2)
+
+            cos_rows = cos_sb[:, c % SEQ_CHUNKS, first : first + PAIR, :]
+            sin_rows = sin_sb[:, c % SEQ_CHUNKS, first : first + PAIR, :]
+            cross_q = work.tile([P, PAIR, Q_COLS], F32)
+            cross_k = work.tile([P, PAIR, KV_COLS], F32)
+            k_rows = k_out[:, first : first + PAIR, :]
+
+            def q_times_cos(i):
+                nc.vector.tensor_tensor(
+                    out=q_out[:, first + i, :].rearrange("p (h d) -> p h d", h=Q_HEADS),
+                    in0=sums_q[i][:].rearrange("p (h d) -> p h d", h=Q_HEADS),
+                    in1=cos_rows[:, i, :].unsqueeze(1).to_broadcast([P, Q_HEADS, HEAD]),
+                    op=MULT,
+                )
+
+            def q_times_sin(i):
+                nc.vector.tensor_tensor(
+                    out=cross_q[:, i, :].rearrange("p (h s d) -> p h s d", h=Q_HEADS, s=2),
+                    in0=sums_q[i][:].rearrange("p (h s d) -> p h s d", h=Q_HEADS, s=2)[:, :, ::-1, :],
+                    in1=sin_rows[:, i, :].rearrange("p (s d) -> p s d", s=2).unsqueeze(1).to_broadcast([P, Q_HEADS, 2, HALF]),
+                    op=MULT,
+                )
+
+            nc.vector.tensor_tensor(
+                out=k_rows.rearrange("p i (h d) -> p i h d", h=KV_HEADS),
+                in0=sums_k[:].rearrange("p i (h d) -> p i h d", h=KV_HEADS),
+                in1=cos_rows.unsqueeze(2).to_broadcast([P, PAIR, KV_HEADS, HEAD]),
+                op=MULT,
+            )
+            nc.vector.tensor_tensor(
+                out=cross_k[:].rearrange("p i (h s d) -> p i h s d", h=KV_HEADS, s=2),
+                in0=sums_k[:].rearrange("p i (h s d) -> p i h s d", h=KV_HEADS, s=2)[:, :, :, ::-1, :],
+                in1=sin_rows.rearrange("p i (s d) -> p i s d", s=2).unsqueeze(2).to_broadcast([P, PAIR, KV_HEADS, 2, HALF]),
+                op=MULT,
+            )
+            q_times_cos(0)
+            q_times_sin(0)
+            q_times_cos(1)
+            if n + 2 < PAIRS:
+                quantise_pair(n + 2)
+            nc.vector.tensor_tensor(out=k_rows, in0=k_rows, in1=cross_k[:], op=ADD)
+            q_times_sin(1)
+            q_rows = q_out[:, first : first + PAIR, :]
+            nc.gpsimd.tensor_tensor(out=q_rows, in0=q_rows, in1=cross_q[:], op=ADD)
             if c == CHUNKS - 1:
                 store_rows(c, first, PAIR)
             elif first + PAIR == CHUNK_TILES:
                 store_rows(c, 0, CHUNK_TILES)
 
+        flip_pair(0)
         quantise_pair(0)
+        flip_pair(1)
         quantise_pair(1)
         for n in range(PAIRS):
             project_pair(n)
-            if n + 2 < PAIRS:
-                quantise_pair(n + 2)

@@ -202,12 +202,12 @@ def tile_attention_pa_t_kernel(
                 in1=sin_rows.rearrange("p i (s d) -> p i s d", s=2).unsqueeze(2).to_broadcast([P, PAIR, KV_HEADS, 2, HALF]),
                 op=MULT,
             )
+            nc.gpsimd.tensor_tensor(out=k_rows, in0=k_rows, in1=cross_k[:], op=ADD)
             q_times_cos(0)
             q_times_sin(0)
             q_times_cos(1)
             if n + 2 < PAIRS:
                 quantise_pair(n + 2)
-            nc.vector.tensor_tensor(out=k_rows, in0=k_rows, in1=cross_k[:], op=ADD)
             q_times_sin(1)
             q_rows = q_out[:, first : first + PAIR, :]
             nc.gpsimd.tensor_tensor(out=q_rows, in0=q_rows, in1=cross_q[:], op=ADD)

@@ -56,8 +56,8 @@ def tile_attention_pa_t_kernel(
         identity = fixed.tile([P, P], F32)
         make_identity(nc, identity[:])
         weights = (
-            (Wq_words, Wq_scales, 0, Q_COLS),
             (Wk_words, Wk_scales, Q_COLS, KV_COLS),
+            (Wq_words, Wq_scales, 0, Q_COLS),
             (Wv_words, Wv_scales, Q_COLS + KV_COLS, KV_COLS),
         )
         for w_words, w_scales, start, width in weights:
@@ -75,26 +75,32 @@ def tile_attention_pa_t_kernel(
             first = PAIR * (n % 2)
             nc.sync.dma_start(out=x_tiles[n][:], in_=x_chunks[n // 2][:, first : first + PAIR, :])
 
-        load_x(0)
-        load_x(1)
-        loaded = 2
+        cos_sb = fixed.tile([P, SEQ_CHUNKS, CHUNK_TILES, HEAD], BF16)
+        sin_sb = fixed.tile([P, SEQ_CHUNKS, CHUNK_TILES, HEAD], BF16)
+        cos_chunks = cos.rearrange("(c p j) d -> p c j d", p=P, j=CHUNK_TILES)
+        sin_chunks = sin.rearrange("(c p j) d -> p c j d", p=P, j=CHUNK_TILES)
+
+        def load_tables(c0, c1):
+            nc.sync.dma_start(out=cos_sb[:, c0:c1], in_=cos_chunks[:, c0:c1])
+            nc.sync.dma_start(out=sin_sb[:, c0:c1], in_=sin_chunks[:, c0:c1])
+
+        def sign_sin(c0, c1):
+            nc.scalar.mul(out=sin_sb[:, c0:c1, :, 0:HALF], in_=sin_sb[:, c0:c1, :, 0:HALF], mul=-1.0)
+
+        for i in range(PAIR):
+            nc.sync.dma_start(out=x_tiles[0][:, i, :], in_=x_chunks[0][:, i, :])
         for w_words, w_scales, start, width in weights:
             rows = w_scales.rearrange("g (q r) n -> r q g n", r=4)
             for r in range(4):
                 nc.sync.dma_start(
                     out=w_planes[r:P:32, :, start : start + width].bitcast(I32), in_=rows[r].bitcast(I32)
                 )
-            load_x(loaded)
-            loaded += 1
-        cos_sb = fixed.tile([P, SEQ_CHUNKS, CHUNK_TILES, HEAD], BF16)
-        sin_sb = fixed.tile([P, SEQ_CHUNKS, CHUNK_TILES, HEAD], BF16)
-        nc.sync.dma_start(out=cos_sb[:], in_=cos.rearrange("(c p j) d -> p c j d", p=P, j=CHUNK_TILES))
-        nc.sync.dma_start(out=sin_sb[:], in_=sin.rearrange("(c p j) d -> p c j d", p=P, j=CHUNK_TILES))
-        for n in range(loaded, PAIRS):
+        load_tables(0, 1)
+        load_x(1)
+        load_x(2)
+        load_tables(1, SEQ_CHUNKS)
+        for n in range(3, PAIRS):
             load_x(n)
-        nc.gpsimd.tensor_scalar(
-            out=sin_sb[:, :, :, 0:HALF], in0=sin_sb[:, :, :, 0:HALF], scalar1=-1.0, scalar2=0.0, op0=MULT, op1=ADD
-        )
 
         grouped_of = {}
         operand_of = {}
@@ -165,6 +171,8 @@ def tile_attention_pa_t_kernel(
             for i in range(PAIR):
                 passes(sums_v[:, i, :], i, Q_COLS + KV_COLS, KV_COLS)
             nc.scalar.copy(out=v_out[:, first : first + PAIR, :], in_=sums_v[:])
+            if n == 0:
+                sign_sin(1, SEQ_CHUNKS)
             if n + 2 < PAIRS:
                 flip_pair(n + 2)
 
@@ -218,6 +226,7 @@ def tile_attention_pa_t_kernel(
 
         flip_pair(0)
         quantise_pair(0)
+        sign_sin(0, 1)
         flip_pair(1)
         quantise_pair(1)
         for n in range(PAIRS):

@@ -28,6 +28,7 @@ CHUNKS = BATCH * SEQ // (P * CHUNK_TILES)
 SEQ_CHUNKS = SEQ // (P * CHUNK_TILES)
 PAIR = 2
 PAIRS = CHUNKS * CHUNK_TILES // PAIR
+ROPE_COLS = PAIR * (Q_COLS + KV_COLS)
 
 FLOPS = 2 * BATCH * SEQ * D * W_COLS
 
@@ -44,7 +45,7 @@ def tile_attention_pa_t_kernel(
 
     with tc.tile_pool(name="fixed", bufs=1) as fixed, tc.tile_pool(name="xin", bufs=PAIRS) as xin, tc.tile_pool(
         name="quant", bufs=2
-    ) as quant, tc.tile_pool(name="work", bufs=3) as work, tc.tile_pool(name="result", bufs=3) as result, tc.psum_pool(
+    ) as quant, tc.tile_pool(name="work", bufs=3) as work, tc.tile_pool(name="result", bufs=4) as result, tc.psum_pool(
         name="flip", bufs=2
     ) as flip, tc.psum_pool(name="qsum", bufs=3) as qsum, tc.psum_pool(name="ksum", bufs=2) as ksum, tc.psum_pool(
         name="vsum", bufs=1
@@ -87,16 +88,20 @@ def tile_attention_pa_t_kernel(
         def sign_sin(c0, c1):
             nc.scalar.mul(out=sin_sb[:, c0:c1, :, 0:HALF], in_=sin_sb[:, c0:c1, :, 0:HALF], mul=-1.0)
 
-        for i in range(PAIR):
-            nc.sync.dma_start(out=x_tiles[0][:, i, :], in_=x_chunks[0][:, i, :])
-        for w_words, w_scales, start, width in weights:
+        def load_scales(w_scales, start, width):
             rows = w_scales.rearrange("g (q r) n -> r q g n", r=4)
             for r in range(4):
                 nc.sync.dma_start(
                     out=w_planes[r:P:32, :, start : start + width].bitcast(I32), in_=rows[r].bitcast(I32)
                 )
-        load_tables(0, 1)
+
+        for i in range(PAIR):
+            nc.sync.dma_start(out=x_tiles[0][:, i, :], in_=x_chunks[0][:, i, :])
+        load_scales(*weights[0][1:])
         load_x(1)
+        load_tables(0, 1)
+        load_scales(*weights[1][1:])
+        load_scales(*weights[2][1:])
         load_x(2)
         load_tables(1, SEQ_CHUNKS)
         for n in range(3, PAIRS):
@@ -104,7 +109,6 @@ def tile_attention_pa_t_kernel(
 
         grouped_of = {}
         operand_of = {}
-        result_of = {}
 
         def flip_pair(n):
             grouped = quant.tile([P, PAIR, PASSES, P, 4], BF16, align_bytes=64)
@@ -130,22 +134,14 @@ def tile_attention_pa_t_kernel(
                 in_=grouped_of[n][:].rearrange("p i g r t -> p (i g r t)"),
             )
 
-        def store_rows(c, first, count):
-            q_out, k_out, v_out = result_of[c]
-            nc.sync.dma_start(out=v_chunks[c][:, first : first + count, :], in_=v_out[:, first : first + count, :])
-            nc.sync.dma_start(out=k_chunks[c][:, first : first + count, :], in_=k_out[:, first : first + count, :])
-            nc.sync.dma_start(out=q_chunks[c][:, first : first + count, :], in_=q_out[:, first : first + count, :])
+        def add_on(engine, straight, cross, start, width):
+            cols = slice(start, start + width)
+            engine.tensor_tensor(out=straight[:, cols], in0=straight[:, cols], in1=cross[:, cols], op=ADD)
 
         def project_pair(n):
             codes, planes = operand_of[n]
             c = n // 2
             first = PAIR * (n % 2)
-            if first == 0:
-                q_new = result.tile([P, CHUNK_TILES, Q_COLS], F32)
-                k_new = result.tile([P, CHUNK_TILES, KV_COLS], F32)
-                v_new = result.tile([P, CHUNK_TILES, KV_COLS], F32)
-                result_of[c] = (q_new, k_new, v_new)
-            q_out, k_out, v_out = result_of[c]
 
             def passes(acc, i, start, width):
                 for g in range(PASSES):
@@ -170,7 +166,9 @@ def tile_attention_pa_t_kernel(
                 passes(sums_qi[:], i, 0, Q_COLS)
             for i in range(PAIR):
                 passes(sums_v[:, i, :], i, Q_COLS + KV_COLS, KV_COLS)
-            nc.scalar.copy(out=v_out[:, first : first + PAIR, :], in_=sums_v[:])
+            v_out = result.tile([P, PAIR, KV_COLS], F32)
+            nc.scalar.copy(out=v_out[:], in_=sums_v[:])
+            nc.sync.dma_start(out=v_chunks[c][:, first : first + PAIR, :], in_=v_out[:])
             if n == 0:
                 sign_sin(1, SEQ_CHUNKS)
             if n + 2 < PAIRS:
@@ -178,51 +176,67 @@ def tile_attention_pa_t_kernel(
 
             cos_rows = cos_sb[:, c % SEQ_CHUNKS, first : first + PAIR, :]
             sin_rows = sin_sb[:, c % SEQ_CHUNKS, first : first + PAIR, :]
-            cross_q = work.tile([P, PAIR, Q_COLS], F32)
-            cross_k = work.tile([P, PAIR, KV_COLS], F32)
-            k_rows = k_out[:, first : first + PAIR, :]
-
-            def q_times_cos(i):
-                nc.vector.tensor_tensor(
-                    out=q_out[:, first + i, :].rearrange("p (h d) -> p h d", h=Q_HEADS),
-                    in0=sums_q[i][:].rearrange("p (h d) -> p h d", h=Q_HEADS),
-                    in1=cos_rows[:, i, :].unsqueeze(1).to_broadcast([P, Q_HEADS, HEAD]),
-                    op=MULT,
-                )
-
-            def q_times_sin(i):
-                nc.vector.tensor_tensor(
-                    out=cross_q[:, i, :].rearrange("p (h s d) -> p h s d", h=Q_HEADS, s=2),
-                    in0=sums_q[i][:].rearrange("p (h s d) -> p h s d", h=Q_HEADS, s=2)[:, :, ::-1, :],
-                    in1=sin_rows[:, i, :].rearrange("p (s d) -> p s d", s=2).unsqueeze(1).to_broadcast([P, Q_HEADS, 2, HALF]),
-                    op=MULT,
-                )
+            straight = result.tile([P, ROPE_COLS], F32)
+            cross = work.tile([P, ROPE_COLS], F32)
+            banks = [(0, PAIR * KV_COLS)] + [(PAIR * KV_COLS + Q_COLS * i, Q_COLS) for i in range(PAIR)]
 
             nc.vector.tensor_tensor(
-                out=k_rows.rearrange("p i (h d) -> p i h d", h=KV_HEADS),
+                out=straight[:, 0 : PAIR * KV_COLS].rearrange("p (i h d) -> p i h d", i=PAIR, h=KV_HEADS),
                 in0=sums_k[:].rearrange("p i (h d) -> p i h d", h=KV_HEADS),
                 in1=cos_rows.unsqueeze(2).to_broadcast([P, PAIR, KV_HEADS, HEAD]),
                 op=MULT,
             )
             nc.vector.tensor_tensor(
-                out=cross_k[:].rearrange("p i (h s d) -> p i h s d", h=KV_HEADS, s=2),
+                out=cross[:, 0 : PAIR * KV_COLS].rearrange("p (i h s d) -> p i h s d", i=PAIR, h=KV_HEADS, s=2),
                 in0=sums_k[:].rearrange("p i (h s d) -> p i h s d", h=KV_HEADS, s=2)[:, :, :, ::-1, :],
                 in1=sin_rows.rearrange("p i (s d) -> p i s d", s=2).unsqueeze(2).to_broadcast([P, PAIR, KV_HEADS, 2, HALF]),
                 op=MULT,
             )
-            nc.gpsimd.tensor_tensor(out=k_rows, in0=k_rows, in1=cross_k[:], op=ADD)
-            q_times_cos(0)
-            q_times_sin(0)
-            q_times_cos(1)
+            if n == 0:
+                add_on(nc.gpsimd, straight, cross, *banks[0])
+            for i in range(PAIR):
+                start, width = banks[1 + i]
+                nc.vector.tensor_tensor(
+                    out=straight[:, start : start + width].rearrange("p (h d) -> p h d", h=Q_HEADS),
+                    in0=sums_q[i][:].rearrange("p (h d) -> p h d", h=Q_HEADS),
+                    in1=cos_rows[:, i, :].unsqueeze(1).to_broadcast([P, Q_HEADS, HEAD]),
+                    op=MULT,
+                )
+                nc.vector.tensor_tensor(
+                    out=cross[:, start : start + width].rearrange("p (h s d) -> p h s d", h=Q_HEADS, s=2),
+                    in0=sums_q[i][:].rearrange("p (h s d) -> p h s d", h=Q_HEADS, s=2)[:, :, ::-1, :],
+                    in1=sin_rows[:, i, :].rearrange("p (s d) -> p s d", s=2).unsqueeze(1).to_broadcast([P, Q_HEADS, 2, HALF]),
+                    op=MULT,
+                )
+                if n == 0:
+                    add_on(nc.gpsimd, straight, cross, start, width)
             if n + 2 < PAIRS:
                 quantise_pair(n + 2)
-            q_times_sin(1)
-            q_rows = q_out[:, first : first + PAIR, :]
-            nc.gpsimd.tensor_tensor(out=q_rows, in0=q_rows, in1=cross_q[:], op=ADD)
-            if c == CHUNKS - 1:
-                store_rows(c, first, PAIR)
-            elif first + PAIR == CHUNK_TILES:
-                store_rows(c, 0, CHUNK_TILES)
+
+            def store_keys():
+                nc.sync.dma_start(
+                    out=k_chunks[c][:, first : first + PAIR, :],
+                    in_=straight[:, 0 : PAIR * KV_COLS].rearrange("p (i m) -> p i m", i=PAIR),
+                )
+
+            def store_queries(i, count):
+                start = banks[1 + i][0]
+                nc.sync.dma_start(
+                    out=q_chunks[c][:, first + i : first + i + count, :],
+                    in_=straight[:, start : start + count * Q_COLS].rearrange("p (i m) -> p i m", i=count),
+                )
+
+            if n == PAIRS - 1:
+                add_on(nc.vector, straight, cross, *banks[0])
+                store_keys()
+                for i in range(PAIR):
+                    add_on(nc.vector, straight, cross, *banks[1 + i])
+                    store_queries(i, 1)
+            else:
+                if n > 0:
+                    add_on(nc.gpsimd, straight, cross, 0, ROPE_COLS)
+                store_keys()
+                store_queries(0, PAIR)
 
         flip_pair(0)
         quantise_pair(0)

@@ -44,8 +44,10 @@ def tile_attention_pa_t_kernel(
     v_chunks = out_2.rearrange("b (c p j) h d -> (b c) p j (h d)", p=P, j=CHUNK_TILES)
 
     with tc.tile_pool(name="fixed", bufs=1) as fixed, tc.tile_pool(name="xin", bufs=PAIRS) as xin, tc.tile_pool(
-        name="quant", bufs=2
-    ) as quant, tc.tile_pool(name="work", bufs=3) as work, tc.tile_pool(name="result", bufs=4) as result, tc.psum_pool(
+        name="group", bufs=2
+    ) as group, tc.tile_pool(name="operand", bufs=3) as operand, tc.tile_pool(name="work", bufs=3) as work, tc.tile_pool(
+        name="result", bufs=3
+    ) as result, tc.psum_pool(
         name="flip", bufs=2
     ) as flip, tc.psum_pool(name="qsum", bufs=3) as qsum, tc.psum_pool(name="ksum", bufs=2) as ksum, tc.psum_pool(
         name="vsum", bufs=1
@@ -99,20 +101,30 @@ def tile_attention_pa_t_kernel(
             nc.sync.dma_start(out=x_tiles[0][:, i, :], in_=x_chunks[0][:, i, :])
         load_scales(*weights[0][1:])
         load_x(1)
+        load_x(2)
         load_tables(0, 1)
         load_scales(*weights[1][1:])
         load_scales(*weights[2][1:])
-        load_x(2)
+        load_x(3)
         load_tables(1, SEQ_CHUNKS)
-        for n in range(3, PAIRS):
+        for n in range(4, PAIRS):
             load_x(n)
 
         grouped_of = {}
         operand_of = {}
+        rope_of = {}
+
+        def quad_of(n):
+            return (n + 1) // 2
+
+        def slot_of(n):
+            return (n + 1) % 2
 
         def flip_pair(n):
-            grouped = quant.tile([P, PAIR, PASSES, P, 4], BF16, align_bytes=64)
-            grouped_of[n] = grouped
+            if quad_of(n) not in grouped_of:
+                grouped_new = group.tile([P, 2, PAIR, PASSES, P, 4], BF16, align_bytes=64)
+                grouped_of[quad_of(n)] = grouped_new
+            grouped = grouped_of[quad_of(n)]
             flipped = []
             for i in range(PAIR):
                 words = x_tiles[n][:, i, :].bitcast(F32)
@@ -122,33 +134,60 @@ def tile_attention_pa_t_kernel(
                     for u in range(2):
                         nc.tensor.transpose(xt[:, g, u, :], words[:, WORDS * g + u : WORDS * (g + 1) : 2], identity[:])
             for i in range(PAIR):
-                nc.scalar.copy(out=grouped[:, i].bitcast(F32), in_=flipped[i][:].rearrange("p g u r -> p g r u"))
+                nc.scalar.copy(
+                    out=grouped[:, slot_of(n), i].bitcast(F32), in_=flipped[i][:].rearrange("p g u r -> p g r u")
+                )
 
-        def quantise_pair(n):
-            codes = quant.tile([P, PAIR, PASSES, P], U32, align_bytes=64)
-            planes = quant.tile([P, PAIR, PASSES, P], U8, align_bytes=64)
-            operand_of[n] = (codes, planes)
+        def quantise_pairs(n, count):
+            if quad_of(n) not in operand_of:
+                codes_new = operand.tile([P, 2, PAIR, PASSES, P], U32, align_bytes=64)
+                planes_new = operand.tile([P, 2, PAIR, PASSES, P], U8, align_bytes=64)
+                operand_of[quad_of(n)] = (codes_new, planes_new)
+            codes, planes = operand_of[quad_of(n)]
+            slots = slice(slot_of(n), slot_of(n) + count)
             nc.vector.quantize_mx(
-                out=codes[:].rearrange("p i g r -> p (i g r)").bitcast(FP8X4),
-                scales=planes[:].rearrange("p i g r -> p (i g r)"),
-                in_=grouped_of[n][:].rearrange("p i g r t -> p (i g r t)"),
+                out=codes[:, slots].rearrange("p a i g r -> p (a i g r)").bitcast(FP8X4),
+                scales=planes[:, slots].rearrange("p a i g r -> p (a i g r)"),
+                in_=grouped_of[quad_of(n)][:, slots].rearrange("p a i g r t -> p (a i g r t)"),
             )
 
-        def add_on(engine, straight, cross, start, width):
+        banks = [(0, PAIR * KV_COLS)] + [(PAIR * KV_COLS + Q_COLS * i, Q_COLS) for i in range(PAIR)]
+
+        def add_on(engine, c, start, width):
+            straight, cross = rope_of[c]
             cols = slice(start, start + width)
             engine.tensor_tensor(out=straight[:, cols], in0=straight[:, cols], in1=cross[:, cols], op=ADD)
 
+        def store_keys(n):
+            straight = rope_of[n // 2][0]
+            first = PAIR * (n % 2)
+            start = ROPE_COLS * (n % 2)
+            nc.sync.dma_start(
+                out=k_chunks[n // 2][:, first : first + PAIR, :],
+                in_=straight[:, start : start + PAIR * KV_COLS].rearrange("p (i m) -> p i m", i=PAIR),
+            )
+
+        def store_queries(n, i, count):
+            straight = rope_of[n // 2][0]
+            first = PAIR * (n % 2) + i
+            start = ROPE_COLS * (n % 2) + banks[1 + i][0]
+            nc.sync.dma_start(
+                out=q_chunks[n // 2][:, first : first + count, :],
+                in_=straight[:, start : start + count * Q_COLS].rearrange("p (i m) -> p i m", i=count),
+            )
+
         def project_pair(n):
-            codes, planes = operand_of[n]
+            codes, planes = operand_of[quad_of(n)]
             c = n // 2
             first = PAIR * (n % 2)
+            base = ROPE_COLS * (n % 2)
 
             def passes(acc, i, start, width):
                 for g in range(PASSES):
                     nc.tensor.matmul_mx(
                         out=acc,
-                        lhsT=codes[:, i, g, :].bitcast(FP8X4),
-                        lhsT_scale=planes[:, i, g, :],
+                        lhsT=codes[:, slot_of(n), i, g, :].bitcast(FP8X4),
+                        lhsT_scale=planes[:, slot_of(n), i, g, :],
                         rhs=w_codes[:, g, start : start + width].bitcast(FP8X4),
                         rhs_scale=w_planes[:, g, start : start + width],
                         start=(g == 0),
@@ -164,6 +203,10 @@ def tile_attention_pa_t_kernel(
                 sums_qi = qsum.tile([P, Q_COLS], F32)
                 sums_q.append(sums_qi)
                 passes(sums_qi[:], i, 0, Q_COLS)
+            if n == 0:
+                flip_pair(2)
+            if n + 3 < PAIRS:
+                flip_pair(n + 3)
             for i in range(PAIR):
                 passes(sums_v[:, i, :], i, Q_COLS + KV_COLS, KV_COLS)
             v_out = result.tile([P, PAIR, KV_COLS], F32)
@@ -171,77 +214,66 @@ def tile_attention_pa_t_kernel(
             nc.sync.dma_start(out=v_chunks[c][:, first : first + PAIR, :], in_=v_out[:])
             if n == 0:
                 sign_sin(1, SEQ_CHUNKS)
-            if n + 2 < PAIRS:
-                flip_pair(n + 2)
 
             cos_rows = cos_sb[:, c % SEQ_CHUNKS, first : first + PAIR, :]
             sin_rows = sin_sb[:, c % SEQ_CHUNKS, first : first + PAIR, :]
-            straight = result.tile([P, ROPE_COLS], F32)
-            cross = work.tile([P, ROPE_COLS], F32)
-            banks = [(0, PAIR * KV_COLS)] + [(PAIR * KV_COLS + Q_COLS * i, Q_COLS) for i in range(PAIR)]
+            if n % 2 == 0:
+                straight_new = result.tile([P, 2 * ROPE_COLS], F32)
+                cross_new = work.tile([P, 2 * ROPE_COLS], F32)
+                rope_of[c] = (straight_new, cross_new)
+            straight, cross = rope_of[c]
 
             nc.vector.tensor_tensor(
-                out=straight[:, 0 : PAIR * KV_COLS].rearrange("p (i h d) -> p i h d", i=PAIR, h=KV_HEADS),
+                out=straight[:, base : base + PAIR * KV_COLS].rearrange("p (i h d) -> p i h d", i=PAIR, h=KV_HEADS),
                 in0=sums_k[:].rearrange("p i (h d) -> p i h d", h=KV_HEADS),
                 in1=cos_rows.unsqueeze(2).to_broadcast([P, PAIR, KV_HEADS, HEAD]),
                 op=MULT,
             )
             nc.vector.tensor_tensor(
-                out=cross[:, 0 : PAIR * KV_COLS].rearrange("p (i h s d) -> p i h s d", i=PAIR, h=KV_HEADS, s=2),
+                out=cross[:, base : base + PAIR * KV_COLS].rearrange("p (i h s d) -> p i h s d", i=PAIR, h=KV_HEADS, s=2),
                 in0=sums_k[:].rearrange("p i (h s d) -> p i h s d", h=KV_HEADS, s=2)[:, :, :, ::-1, :],
                 in1=sin_rows.rearrange("p i (s d) -> p i s d", s=2).unsqueeze(2).to_broadcast([P, PAIR, KV_HEADS, 2, HALF]),
                 op=MULT,
             )
             if n == 0:
-                add_on(nc.gpsimd, straight, cross, *banks[0])
+                add_on(nc.gpsimd, c, *banks[0])
+                quantise_pairs(1, 1)
             for i in range(PAIR):
                 start, width = banks[1 + i]
                 nc.vector.tensor_tensor(
-                    out=straight[:, start : start + width].rearrange("p (h d) -> p h d", h=Q_HEADS),
+                    out=straight[:, base + start : base + start + width].rearrange("p (h d) -> p h d", h=Q_HEADS),
                     in0=sums_q[i][:].rearrange("p (h d) -> p h d", h=Q_HEADS),
                     in1=cos_rows[:, i, :].unsqueeze(1).to_broadcast([P, Q_HEADS, HEAD]),
                     op=MULT,
                 )
                 nc.vector.tensor_tensor(
-                    out=cross[:, start : start + width].rearrange("p (h s d) -> p h s d", h=Q_HEADS, s=2),
+                    out=cross[:, base + start : base + start + width].rearrange("p (h s d) -> p h s d", h=Q_HEADS, s=2),
                     in0=sums_q[i][:].rearrange("p (h s d) -> p h s d", h=Q_HEADS, s=2)[:, :, ::-1, :],
                     in1=sin_rows[:, i, :].rearrange("p (s d) -> p s d", s=2).unsqueeze(1).to_broadcast([P, Q_HEADS, 2, HALF]),
                     op=MULT,
                 )
                 if n == 0:
-                    add_on(nc.gpsimd, straight, cross, start, width)
-            if n + 2 < PAIRS:
-                quantise_pair(n + 2)
-
-            def store_keys():
-                nc.sync.dma_start(
-                    out=k_chunks[c][:, first : first + PAIR, :],
-                    in_=straight[:, 0 : PAIR * KV_COLS].rearrange("p (i m) -> p i m", i=PAIR),
-                )
-
-            def store_queries(i, count):
-                start = banks[1 + i][0]
-                nc.sync.dma_start(
-                    out=q_chunks[c][:, first + i : first + i + count, :],
-                    in_=straight[:, start : start + count * Q_COLS].rearrange("p (i m) -> p i m", i=count),
-                )
+                    add_on(nc.gpsimd, c, start, width)
+            if n == 0:
+                quantise_pairs(2, 1)
+            elif n % 2 == 1 and n + 2 < PAIRS:
+                quantise_pairs(n + 2, min(2, PAIRS - (n + 2)))
 
             if n == PAIRS - 1:
-                add_on(nc.vector, straight, cross, *banks[0])
-                store_keys()
+                add_on(nc.vector, c, base + banks[0][0], banks[0][1])
+                store_keys(n)
                 for i in range(PAIR):
-                    add_on(nc.vector, straight, cross, *banks[1 + i])
-                    store_queries(i, 1)
+                    add_on(nc.vector, c, base + banks[1 + i][0], banks[1 + i][1])
+                    store_queries(n, i, 1)
             else:
                 if n > 0:
-                    add_on(nc.gpsimd, straight, cross, 0, ROPE_COLS)
-                store_keys()
-                store_queries(0, PAIR)
+                    add_on(nc.gpsimd, c, base, ROPE_COLS)
+                store_keys(n)
+                store_queries(n, 0, PAIR)
 
         flip_pair(0)
-        quantise_pair(0)
+        quantise_pairs(0, 1)
         sign_sin(0, 1)
         flip_pair(1)
-        quantise_pair(1)
         for n in range(PAIRS):
             project_pair(n)

@@ -30,6 +30,8 @@ PAIR = 2
 PAIRS = CHUNKS * CHUNK_TILES // PAIR
 ROPE_COLS = PAIR * (Q_COLS + KV_COLS)
 
+PE_COLS = HEAD
+
 FLOPS = 2 * BATCH * SEQ * D * W_COLS
 
 
@@ -49,9 +51,9 @@ def tile_attention_pa_t_kernel(
         name="result", bufs=3
     ) as result, tc.psum_pool(
         name="flip", bufs=2
-    ) as flip, tc.psum_pool(name="qsum", bufs=3) as qsum, tc.psum_pool(name="ksum", bufs=2) as ksum, tc.psum_pool(
+    ) as flip, tc.psum_pool(name="qsum", bufs=3) as qsum, tc.psum_pool(name="ksum", bufs=1) as ksum, tc.psum_pool(
         name="vsum", bufs=1
-    ) as vsum, tc.manual_schedule():
+    ) as vsum, tc.psum_pool(name="esum", bufs=1) as esum, tc.manual_schedule():
         w_codes = fixed.tile([P, PASSES, W_COLS], U32, align_bytes=64)
         w_planes = fixed.tile([P, PASSES, W_COLS], U8, align_bytes=64)
         nc.vector.memset(w_planes[:].rearrange("p g n -> p (g n)").bitcast(I32), 0)
@@ -176,6 +178,14 @@ def tile_attention_pa_t_kernel(
                 in_=straight[:, start : start + count * Q_COLS].rearrange("p (i m) -> p i m", i=count),
             )
 
+        def add_on_tensor_engine(n):
+            straight, cross = rope_of[n // 2]
+            cols = slice(ROPE_COLS * (n % 2) + ROPE_COLS - PE_COLS, ROPE_COLS * (n % 2) + ROPE_COLS)
+            total = esum.tile([P, PE_COLS], F32)
+            nc.tensor.matmul(out=total[:], lhsT=identity[:], rhs=straight[:, cols], start=True, stop=False)
+            nc.tensor.matmul(out=total[:], lhsT=identity[:], rhs=cross[:, cols], start=False, stop=True)
+            nc.scalar.copy(out=straight[:, cols], in_=total[:])
+
         def project_pair(n):
             codes, planes = operand_of[quad_of(n)]
             c = n // 2
@@ -212,6 +222,9 @@ def tile_attention_pa_t_kernel(
             v_out = result.tile([P, PAIR, KV_COLS], F32)
             nc.scalar.copy(out=v_out[:], in_=sums_v[:])
             nc.sync.dma_start(out=v_chunks[c][:, first : first + PAIR, :], in_=v_out[:])
+            if n >= 2:
+                add_on_tensor_engine(n - 1)
+                store_queries(n - 1, 0, PAIR)
             if n == 0:
                 sign_sin(1, SEQ_CHUNKS)
 
@@ -267,9 +280,10 @@ def tile_attention_pa_t_kernel(
                     store_queries(n, i, 1)
             else:
                 if n > 0:
-                    add_on(nc.gpsimd, c, base, ROPE_COLS)
+                    add_on(nc.gpsimd, c, base, ROPE_COLS - PE_COLS)
                 store_keys(n)
-                store_queries(n, 0, PAIR)
+                if n == 0:
+                    store_queries(n, 0, PAIR)
 
         flip_pair(0)
         quantise_pairs(0, 1)

@@ -92,6 +92,13 @@ def tile_attention_pa_t_kernel(
         def sign_sin(c0, c1):
             nc.scalar.mul(out=sin_sb[:, c0:c1, :, 0:HALF], in_=sin_sb[:, c0:c1, :, 0:HALF], mul=-1.0)
 
+        cos_wide = fixed.tile([P, SEQ_CHUNKS, CHUNK_TILES, HEAD], F32)
+        sin_wide = fixed.tile([P, SEQ_CHUNKS, CHUNK_TILES, HEAD], F32)
+
+        def widen_tables(c):
+            nc.scalar.copy(out=cos_wide[:, c], in_=cos_sb[:, c])
+            nc.scalar.copy(out=sin_wide[:, c], in_=sin_sb[:, c])
+
         def load_scales(w_scales, start, width):
             rows = w_scales.rearrange("g (q r) n -> r q g n", r=4)
             for r in range(4):
@@ -227,9 +234,15 @@ def tile_attention_pa_t_kernel(
                 store_queries(n - 1, 0, PAIR)
             if n == 0:
                 sign_sin(1, SEQ_CHUNKS)
+            if n % 2 == 0 and c < SEQ_CHUNKS:
+                widen_tables((c + 1) % SEQ_CHUNKS)
 
-            cos_rows = cos_sb[:, c % SEQ_CHUNKS, first : first + PAIR, :]
-            sin_rows = sin_sb[:, c % SEQ_CHUNKS, first : first + PAIR, :]
+            if c == 0:
+                cos_rows = cos_sb[:, 0, first : first + PAIR, :]
+                sin_rows = sin_sb[:, 0, first : first + PAIR, :]
+            else:
+                cos_rows = cos_wide[:, c % SEQ_CHUNKS, first : first + PAIR, :]
+                sin_rows = sin_wide[:, c % SEQ_CHUNKS, first : first + PAIR, :]
             if n % 2 == 0:
                 straight_new = result.tile([P, 2 * ROPE_COLS], F32)
                 cross_new = work.tile([P, 2 * ROPE_COLS], F32)

import concourse.mybir as mybir
from concourse.masks import make_identity

F32 = mybir.dt.float32
BF16 = mybir.dt.bfloat16
I32 = mybir.dt.int32
U32 = mybir.dt.uint32
U8 = mybir.dt.uint8
FP8X4 = mybir.dt.float8_e4m3fn_x4
MULT = mybir.AluOpType.mult
ADD = mybir.AluOpType.add

P = 128
BATCH, SEQ, D = 2, 2048, 1024
HEAD = 128
HALF = HEAD // 2
Q_HEADS, KV_HEADS = 4, 2
Q_COLS = Q_HEADS * HEAD
KV_COLS = KV_HEADS * HEAD
W_COLS = Q_COLS + 2 * KV_COLS
BANK = 512
K_PASS = 4 * P
PASSES = D // K_PASS
WORDS = K_PASS // 2

CHUNK_TILES = 4
CHUNKS = BATCH * SEQ // (P * CHUNK_TILES)
SEQ_CHUNKS = SEQ // (P * CHUNK_TILES)
PAIR = 2
PAIRS = CHUNKS * CHUNK_TILES // PAIR
ROPE_COLS = PAIR * (Q_COLS + KV_COLS)

PE_COLS = HEAD

FLOPS = 2 * BATCH * SEQ * D * W_COLS


def tile_attention_pa_t_kernel(
    tc, x, cos, sin, Wq_words, Wq_scales, Wk_words, Wk_scales, Wv_words, Wv_scales, out_0, out_1, out_2
):
    nc = tc.nc

    x_chunks = x.rearrange("b (c p j) d -> (b c) p j d", p=P, j=CHUNK_TILES)
    q_chunks = out_0.rearrange("b (c p j) h d -> (b c) p j (h d)", p=P, j=CHUNK_TILES)
    k_chunks = out_1.rearrange("b (c p j) h d -> (b c) p j (h d)", p=P, j=CHUNK_TILES)
    v_chunks = out_2.rearrange("b (c p j) h d -> (b c) p j (h d)", p=P, j=CHUNK_TILES)

    with tc.tile_pool(name="fixed", bufs=1) as fixed, tc.tile_pool(name="xin", bufs=PAIRS) as xin, tc.tile_pool(
        name="group", bufs=2
    ) as group, tc.tile_pool(name="operand", bufs=3) as operand, tc.tile_pool(name="work", bufs=3) as work, tc.tile_pool(
        name="result", bufs=3
    ) as result, tc.psum_pool(
        name="flip", bufs=2
    ) as flip, tc.psum_pool(name="qsum", bufs=3) as qsum, tc.psum_pool(name="ksum", bufs=1) as ksum, tc.psum_pool(
        name="vsum", bufs=1
    ) as vsum, tc.psum_pool(name="esum", bufs=1) as esum, tc.manual_schedule():
        w_codes = fixed.tile([P, PASSES, W_COLS], U32, align_bytes=64)
        w_planes = fixed.tile([P, PASSES, W_COLS], U8, align_bytes=64)
        nc.vector.memset(w_planes[:].rearrange("p g n -> p (g n)").bitcast(I32), 0)

        identity = fixed.tile([P, P], F32)
        make_identity(nc, identity[:])
        weights = (
            (Wk_words, Wk_scales, Q_COLS, KV_COLS),
            (Wq_words, Wq_scales, 0, Q_COLS),
            (Wv_words, Wv_scales, Q_COLS + KV_COLS, KV_COLS),
        )
        for w_words, w_scales, start, width in weights:
            nc.gpsimd.dma_start(
                out=w_codes[:, :, start : start + width].bitcast(F32),
                in_=w_words.rearrange("g p n t -> p g (n t)").bitcast(F32),
            )

        x_tiles = []
        for n in range(PAIRS):
            x_tile = xin.tile([P, PAIR, D], BF16)
            x_tiles.append(x_tile)

        def load_x(n):
            first = PAIR * (n % 2)
            nc.sync.dma_start(out=x_tiles[n][:], in_=x_chunks[n // 2][:, first : first + PAIR, :])

        cos_sb = fixed.tile([P, SEQ_CHUNKS, CHUNK_TILES, HEAD], BF16)
        sin_sb = fixed.tile([P, SEQ_CHUNKS, CHUNK_TILES, HEAD], BF16)
        cos_chunks = cos.rearrange("(c p j) d -> p c j d", p=P, j=CHUNK_TILES)
        sin_chunks = sin.rearrange("(c p j) d -> p c j d", p=P, j=CHUNK_TILES)

        def load_tables(c0, c1):
            nc.sync.dma_start(out=cos_sb[:, c0:c1], in_=cos_chunks[:, c0:c1])
            nc.sync.dma_start(out=sin_sb[:, c0:c1], in_=sin_chunks[:, c0:c1])

        def sign_sin(c0, c1):
            nc.scalar.mul(out=sin_sb[:, c0:c1, :, 0:HALF], in_=sin_sb[:, c0:c1, :, 0:HALF], mul=-1.0)

        cos_wide = fixed.tile([P, SEQ_CHUNKS, CHUNK_TILES, HEAD], F32)
        sin_wide = fixed.tile([P, SEQ_CHUNKS, CHUNK_TILES, HEAD], F32)

        def widen_tables(c):
            nc.scalar.copy(out=cos_wide[:, c], in_=cos_sb[:, c])
            nc.scalar.copy(out=sin_wide[:, c], in_=sin_sb[:, c])

        def load_scales(w_scales, start, width):
            rows = w_scales.rearrange("g (q r) n -> r q g n", r=4)
            for r in range(4):
                nc.sync.dma_start(
                    out=w_planes[r:P:32, :, start : start + width].bitcast(I32), in_=rows[r].bitcast(I32)
                )

        for i in range(PAIR):
            nc.sync.dma_start(out=x_tiles[0][:, i, :], in_=x_chunks[0][:, i, :])
        load_scales(*weights[0][1:])
        load_x(1)
        load_x(2)
        load_tables(0, 1)
        load_scales(*weights[1][1:])
        load_scales(*weights[2][1:])
        load_x(3)
        load_tables(1, SEQ_CHUNKS)
        for n in range(4, PAIRS):
            load_x(n)

        grouped_of = {}
        operand_of = {}
        rope_of = {}

        def quad_of(n):
            return (n + 1) // 2

        def slot_of(n):
            return (n + 1) % 2

        def flip_pair(n):
            if quad_of(n) not in grouped_of:
                grouped_new = group.tile([P, 2, PAIR, PASSES, P, 4], BF16, align_bytes=64)
                grouped_of[quad_of(n)] = grouped_new
            grouped = grouped_of[quad_of(n)]
            flipped = []
            for i in range(PAIR):
                words = x_tiles[n][:, i, :].bitcast(F32)
                xt = flip.tile([P, PASSES, 2, P], F32)
                flipped.append(xt)
                for g in range(PASSES):
                    for u in range(2):
                        nc.tensor.transpose(xt[:, g, u, :], words[:, WORDS * g + u : WORDS * (g + 1) : 2], identity[:])
            for i in range(PAIR):
                nc.scalar.copy(
                    out=grouped[:, slot_of(n), i].bitcast(F32), in_=flipped[i][:].rearrange("p g u r -> p g r u")
                )

        def quantise_pairs(n, count):
            if quad_of(n) not in operand_of:
                codes_new = operand.tile([P, 2, PAIR, PASSES, P], U32, align_bytes=64)
                planes_new = operand.tile([P, 2, PAIR, PASSES, P], U8, align_bytes=64)
                operand_of[quad_of(n)] = (codes_new, planes_new)
            codes, planes = operand_of[quad_of(n)]
            slots = slice(slot_of(n), slot_of(n) + count)
            nc.vector.quantize_mx(
                out=codes[:, slots].rearrange("p a i g r -> p (a i g r)").bitcast(FP8X4),
                scales=planes[:, slots].rearrange("p a i g r -> p (a i g r)"),
                in_=grouped_of[quad_of(n)][:, slots].rearrange("p a i g r t -> p (a i g r t)"),
            )

        banks = [(0, PAIR * KV_COLS)] + [(PAIR * KV_COLS + Q_COLS * i, Q_COLS) for i in range(PAIR)]

        def add_on(engine, c, start, width):
            straight, cross = rope_of[c]
            cols = slice(start, start + width)
            engine.tensor_tensor(out=straight[:, cols], in0=straight[:, cols], in1=cross[:, cols], op=ADD)

        def store_keys(n):
            straight = rope_of[n // 2][0]
            first = PAIR * (n % 2)
            start = ROPE_COLS * (n % 2)
            nc.sync.dma_start(
                out=k_chunks[n // 2][:, first : first + PAIR, :],
                in_=straight[:, start : start + PAIR * KV_COLS].rearrange("p (i m) -> p i m", i=PAIR),
            )

        def store_queries(n, i, count):
            straight = rope_of[n // 2][0]
            first = PAIR * (n % 2) + i
            start = ROPE_COLS * (n % 2) + banks[1 + i][0]
            nc.sync.dma_start(
                out=q_chunks[n // 2][:, first : first + count, :],
                in_=straight[:, start : start + count * Q_COLS].rearrange("p (i m) -> p i m", i=count),
            )

        def add_on_tensor_engine(n):
            straight, cross = rope_of[n // 2]
            cols = slice(ROPE_COLS * (n % 2) + ROPE_COLS - PE_COLS, ROPE_COLS * (n % 2) + ROPE_COLS)
            total = esum.tile([P, PE_COLS], F32)
            nc.tensor.matmul(out=total[:], lhsT=identity[:], rhs=straight[:, cols], start=True, stop=False)
            nc.tensor.matmul(out=total[:], lhsT=identity[:], rhs=cross[:, cols], start=False, stop=True)
            nc.scalar.copy(out=straight[:, cols], in_=total[:])

        def project_pair(n):
            codes, planes = operand_of[quad_of(n)]
            c = n // 2
            first = PAIR * (n % 2)
            base = ROPE_COLS * (n % 2)

            def passes(acc, i, start, width):
                for g in range(PASSES):
                    nc.tensor.matmul_mx(
                        out=acc,
                        lhsT=codes[:, slot_of(n), i, g, :].bitcast(FP8X4),
                        lhsT_scale=planes[:, slot_of(n), i, g, :],
                        rhs=w_codes[:, g, start : start + width].bitcast(FP8X4),
                        rhs_scale=w_planes[:, g, start : start + width],
                        start=(g == 0),
                        stop=(g == PASSES - 1),
                    )

            sums_k = ksum.tile([P, PAIR, KV_COLS], F32)
            sums_v = vsum.tile([P, PAIR, KV_COLS], F32)
            sums_q = []
            for i in range(PAIR):
                passes(sums_k[:, i, :], i, Q_COLS, KV_COLS)
            for i in range(PAIR):
                sums_qi = qsum.tile([P, Q_COLS], F32)
                sums_q.append(sums_qi)
                passes(sums_qi[:], i, 0, Q_COLS)
            if n == 0:
                flip_pair(2)
            if n + 3 < PAIRS:
                flip_pair(n + 3)
            for i in range(PAIR):
                passes(sums_v[:, i, :], i, Q_COLS + KV_COLS, KV_COLS)
            v_out = result.tile([P, PAIR, KV_COLS], F32)
            nc.scalar.copy(out=v_out[:], in_=sums_v[:])
            nc.sync.dma_start(out=v_chunks[c][:, first : first + PAIR, :], in_=v_out[:])
            if n >= 2:
                add_on_tensor_engine(n - 1)
                store_queries(n - 1, 0, PAIR)
            if n == 0:
                sign_sin(1, SEQ_CHUNKS)
            if n % 2 == 0 and c < SEQ_CHUNKS:
                widen_tables((c + 1) % SEQ_CHUNKS)

            if c == 0:
                cos_rows = cos_sb[:, 0, first : first + PAIR, :]
                sin_rows = sin_sb[:, 0, first : first + PAIR, :]
            else:
                cos_rows = cos_wide[:, c % SEQ_CHUNKS, first : first + PAIR, :]
                sin_rows = sin_wide[:, c % SEQ_CHUNKS, first : first + PAIR, :]
            if n % 2 == 0:
                straight_new = result.tile([P, 2 * ROPE_COLS], F32)
                cross_new = work.tile([P, 2 * ROPE_COLS], F32)
                rope_of[c] = (straight_new, cross_new)
            straight, cross = rope_of[c]

            nc.vector.tensor_tensor(
                out=straight[:, base : base + PAIR * KV_COLS].rearrange("p (i h d) -> p i h d", i=PAIR, h=KV_HEADS),
                in0=sums_k[:].rearrange("p i (h d) -> p i h d", h=KV_HEADS),
                in1=cos_rows.unsqueeze(2).to_broadcast([P, PAIR, KV_HEADS, HEAD]),
                op=MULT,
            )
            nc.vector.tensor_tensor(
                out=cross[:, base : base + PAIR * KV_COLS].rearrange("p (i h s d) -> p i h s d", i=PAIR, h=KV_HEADS, s=2),
                in0=sums_k[:].rearrange("p i (h s d) -> p i h s d", h=KV_HEADS, s=2)[:, :, :, ::-1, :],
                in1=sin_rows.rearrange("p i (s d) -> p i s d", s=2).unsqueeze(2).to_broadcast([P, PAIR, KV_HEADS, 2, HALF]),
                op=MULT,
            )
            if n == 0:
                add_on(nc.gpsimd, c, *banks[0])
                quantise_pairs(1, 1)
            for i in range(PAIR):
                start, width = banks[1 + i]
                nc.vector.tensor_tensor(
                    out=straight[:, base + start : base + start + width].rearrange("p (h d) -> p h d", h=Q_HEADS),
                    in0=sums_q[i][:].rearrange("p (h d) -> p h d", h=Q_HEADS),
                    in1=cos_rows[:, i, :].unsqueeze(1).to_broadcast([P, Q_HEADS, HEAD]),
                    op=MULT,
                )
                nc.vector.tensor_tensor(
                    out=cross[:, base + start : base + start + width].rearrange("p (h s d) -> p h s d", h=Q_HEADS, s=2),
                    in0=sums_q[i][:].rearrange("p (h s d) -> p h s d", h=Q_HEADS, s=2)[:, :, ::-1, :],
                    in1=sin_rows[:, i, :].rearrange("p (s d) -> p s d", s=2).unsqueeze(1).to_broadcast([P, Q_HEADS, 2, HALF]),
                    op=MULT,
                )
                if n == 0:
                    add_on(nc.gpsimd, c, start, width)
            if n == 0:
                quantise_pairs(2, 1)
            elif n % 2 == 1 and n + 2 < PAIRS:
                quantise_pairs(n + 2, min(2, PAIRS - (n + 2)))

            if n == PAIRS - 1:
                add_on(nc.vector, c, base + banks[0][0], banks[0][1])
                store_keys(n)
                for i in range(PAIR):
                    add_on(nc.vector, c, base + banks[1 + i][0], banks[1 + i][1])
                    store_queries(n, i, 1)
            else:
                if n > 0:
                    add_on(nc.gpsimd, c, base, ROPE_COLS - PE_COLS)
                store_keys(n)
                if n == 0:
                    store_queries(n, 0, PAIR)

        flip_pair(0)
        quantise_pairs(0, 1)
        sign_sin(0, 1)
        flip_pair(1)
        for n in range(PAIRS):
            project_pair(n)
